import numpy as np
import ml_dtypes


def mxq(x, axis, fmt="e4m3"):
    dtype, down = {"e4m3": (ml_dtypes.float8_e4m3fn, 7), "e5m2": (ml_dtypes.float8_e5m2, 14)}[fmt]
    v = np.moveaxis(np.asarray(x, np.float32).astype(ml_dtypes.bfloat16).astype(np.float64), axis, -1)
    blocks = v.reshape(v.shape[:-1] + (-1, 32))
    amax = np.abs(blocks).max(-1, keepdims=True)
    byte = np.maximum(np.where(amax > 0, np.frexp(amax)[1] - 1 + 127, 0) - down, 1)
    scale = np.exp2(byte - 127.0)
    codes = (blocks / scale).astype(np.float32).astype(dtype).astype(np.float64)
    return np.moveaxis((codes * scale).reshape(v.shape), -1, axis)


WIDE = False


def mx_kscale(k):
    if not WIDE:
        return np.ones(k)
    levels = np.array([10, -10, 5, -5, 0])
    a = np.random.permutation(np.resize(levels, k // 512 * 4)).reshape(k // 512, 4)
    idx = np.arange(k)
    return np.exp2(a[idx // 512, idx % 128 // 32])


BF16 = ml_dtypes.bfloat16


def bf(x):
    return np.asarray(x, np.float32).astype(BF16)


def f64(x):
    return np.asarray(x).astype(np.float64)


B, S, E, H, HKV, D, F, M0, M1 = 1, 512, 1536, 32, 4, 128, 8192, 48, 40
M2 = D - M0 - M1
ROPE_BASE = 1000000.0
EPS = 1e-6


def rms_norm(v, w):
    return w * (v / np.sqrt(np.mean(v * v, axis=-1, keepdims=True) + EPS))


def mrope_cos_sin():
    t = np.arange(S, dtype=np.float64)
    parts = []
    for sd in (M0, M1, M2):
        inv_freq = 1.0 / ROPE_BASE ** (np.arange(0, sd, 2, dtype=np.float64) / sd)
        freqs = t[:, None] * inv_freq[None, :]
        parts.append(np.concatenate([freqs, freqs], -1))
    emb = np.concatenate(parts, -1)
    return np.cos(emb), np.sin(emb)


def rotate_half(v):
    d = D // 2
    return np.concatenate([-v[..., d:], v[..., :d]], -1)


def setup_inputs():
    s = mx_kscale(E)
    row = 0.5 + 1.5 * np.random.random_sample((B, S, 1))
    return {"x": bf(np.random.standard_normal((B, S, E)) * row),
            "ln1_w": bf((1.0 + 0.1 * np.random.standard_normal(E)) * s),
            "wq": bf(np.random.standard_normal((H * D, E)) / np.sqrt(E) / s),
            "wk": bf(np.random.standard_normal((HKV * D, E)) / np.sqrt(E) / s),
            "wv": bf(np.random.standard_normal((HKV * D, E)) / np.sqrt(E) / s),
            "q_norm_w": bf(1.0 + 0.1 * np.random.standard_normal(D)),
            "k_norm_w": bf(1.0 + 0.1 * np.random.standard_normal(D))}


def reference(x, ln1_w, wq, wk, wv, q_norm_w, k_norm_w):
    hq = mxq(rms_norm(f64(x), f64(ln1_w)), 2, "e4m3")
    q = (hq @ mxq(f64(wq), 1, "e4m3").T).reshape(B, S, H, D).transpose(0, 2, 1, 3)
    k = (hq @ mxq(f64(wk), 1, "e4m3").T).reshape(B, S, HKV, D).transpose(0, 2, 1, 3)
    v = (hq @ mxq(f64(wv), 1, "e4m3").T).reshape(B, S, HKV, D).transpose(0, 2, 1, 3)
    q = rms_norm(q, f64(q_norm_w))
    k = rms_norm(k, f64(k_norm_w))
    cos, sin = mrope_cos_sin()
    q = q * cos + rotate_half(q) * sin
    k = k * cos + rotate_half(k) * sin
    return q, k, v

@@ -1,0 +1,454 @@
+import math
+from contextlib import ExitStack
+
+import concourse.mybir as mybir
+from concourse.masks import make_identity
+
+F32 = mybir.dt.float32
+BF16 = mybir.dt.bfloat16
+I32 = mybir.dt.int32
+U32 = mybir.dt.uint32
+U8 = mybir.dt.uint8
+FP8X4 = mybir.dt.float8_e4m3fn_x4
+ACT = mybir.ActivationFunctionType
+ALU = mybir.AluOpType
+
+P = 128
+S = 512
+E = 1536
+D = 128
+NA = S // P
+NG = E // 512
+NC = 10
+NF = 44
+ROPE_BASE = 1000000.0
+EPS = 1e-6
+TWO_PI = 2.0 * math.pi
+RAW_BUFS = 5
+MANUAL = True
+
+FLOPS = 2 * S * E * (NC * 512)
+
+
+def tile_selectivetransformerlayer_pa_kernel(
+    tc, x, ln1_w, wq, wk, wv, q_norm_w, k_norm_w, out_0, out_1, out_2
+):
+    nc = tc.nc
+    with ExitStack() as ctx:
+        const = ctx.enter_context(tc.tile_pool(name="const", bufs=1))
+        rawp = ctx.enter_context(tc.tile_pool(name="rawp", bufs=RAW_BUFS))
+        codep = ctx.enter_context(tc.tile_pool(name="codep", bufs=3))
+        grp = ctx.enter_context(tc.tile_pool(name="grp", bufs=3))
+        small = ctx.enter_context(tc.tile_pool(name="small", bufs=4))
+        ep = ctx.enter_context(tc.tile_pool(name="ep", bufs=3))
+        outp = ctx.enter_context(tc.tile_pool(name="outp", bufs=4))
+        psum_t = ctx.enter_context(tc.psum_pool(name="psum_t", bufs=4))
+        psum_a = ctx.enter_context(tc.psum_pool(name="psum_a", bufs=4))
+        if MANUAL:
+            ctx.enter_context(tc.manual_schedule())
+
+        x_v = x.rearrange("o (a p) k -> p (o a) k", p=P)
+        wq_v = wq.rearrange("(c b p) k -> c p b k", b=4, p=P)
+        wk_v = wk.rearrange("(b p) k -> p b k", p=P)
+        wv_v = wv.rearrange("(b p) k -> p b k", p=P)
+        o0_v = out_0.rearrange("o h (a p) d -> p (o h) a d", p=P)
+        o1_v = out_1.rearrange("o h (a p) d -> p (o h) a d", p=P)
+        o2_v = out_2.rearrange("o h (a p) d -> p (o h) a d", p=P)
+
+        def w_src(c):
+            if c < 8:
+                return wq_v[c]
+            if c == 8:
+                return wk_v
+            return wv_v
+
+        def o_dst(c, a):
+            if c < 8:
+                return o0_v[:, 4 * c : 4 * c + 4, a, :]
+            if c == 8:
+                return o1_v[:, :, a, :]
+            return o2_v[:, :, a, :]
+
+        wrow = const.tile([P, E + 2 * D], BF16)
+        nc.vector.memset(wrow[:], 0.0)
+        ones_b = const.tile([P, P], BF16)
+        nc.vector.memset(ones_b[:], 1.0)
+        warm = const.tile([P, 1], F32)
+        nc.vector.memset(warm[:], 0.0)
+        eps_t = const.tile([P, 1], F32)
+        nc.vector.memset(eps_t[:], EPS)
+        neghalf = const.tile([P, 1], F32)
+        nc.vector.memset(neghalf[:], -0.5)
+
+        nc.sync.dma_start(out=wrow[0:1, 0:E], in_=ln1_w.unsqueeze(0))
+        nc.sync.dma_start(out=wrow[0:1, E : E + D], in_=q_norm_w.unsqueeze(0))
+        nc.sync.dma_start(out=wrow[0:1, E + D : E + 2 * D], in_=k_norm_w.unsqueeze(0))
+        x_sb = const.tile([P, NA, E], BF16)
+        for a in range(NA):
+            nc.sync.dma_start(out=x_sb[:, a, :], in_=x_v[:, a, :])
+
+        raw = {}
+
+        def load_w(c):
+            w_raw = rawp.tile([P, 4, E], BF16, tag="w_raw")
+            nc.sync.dma_start(out=w_raw[:], in_=w_src(c))
+            raw[c] = w_raw
+
+        for c in range(RAW_BUFS):
+            load_w(c)
+
+        tpos_i = const.tile([P, NA], I32)
+        nc.gpsimd.iota(tpos_i[:], pattern=[[P, NA]], base=0, channel_multiplier=1)
+        ident_f = const.tile([P, P], F32)
+        make_identity(nc, ident_f[:])
+        ident_b = const.tile([P, P], BF16)
+        make_identity(nc, ident_b[:])
+        warm2 = const.tile([P, 1], F32)
+        nc.scalar.activation(out=warm2[:], in_=warm[:], func=ACT.Sin)
+
+        tpos = const.tile([P, NA], F32)
+        nc.vector.tensor_copy(out=tpos[:], in_=tpos_i[:])
+        turns = const.tile([P, 2, NF, NA], F32)
+        for j in range(NF):
+            if j < 24:
+                cj = ROPE_BASE ** (-2.0 * j / 48.0) / TWO_PI
+            else:
+                cj = ROPE_BASE ** (-2.0 * (j - 24) / 40.0) / TWO_PI
+            nc.vector.tensor_scalar_mul(out=turns[:, 1, j, :], in0=tpos[:], scalar1=cj)
+        nc.vector.tensor_scalar_add(out=turns[:, 0], in0=turns[:, 1], scalar1=0.25)
+        NT = 2 * NF * NA
+        turns_f = turns[:].rearrange("p s j a -> p (s j a)")
+        whole_i = const.tile([P, NT], I32)
+        nc.vector.tensor_copy(out=whole_i[:], in_=turns_f)
+        whole = const.tile([P, NT], F32)
+        nc.vector.tensor_copy(out=whole[:], in_=whole_i[:])
+        frac = const.tile([P, NT], F32)
+        nc.vector.tensor_tensor(out=frac[:], in0=turns_f, in1=whole[:], op=ALU.subtract)
+        fneg = const.tile([P, NT], F32)
+        nc.vector.scalar_tensor_tensor(
+            out=fneg[:], in0=frac[:], scalar=0.5, in1=frac[:], op0=ALU.is_gt, op1=ALU.subtract
+        )
+        fr = const.tile([P, 2, NF, NA], F32)
+        nc.vector.scalar_tensor_tensor(
+            out=fr[:].rearrange("p s j a -> p (s j a)"),
+            in0=fneg[:],
+            scalar=0.5,
+            in1=fneg[:],
+            op0=ALU.is_gt,
+            op1=ALU.subtract,
+        )
+
+        wb = []
+        for i in range(4):
+            n = 512 if i < 3 else 2 * D
+            wbi = psum_a.tile([P, 512], F32, tag="acc", name="wb%d" % i)
+            nc.tensor.matmul(
+                out=wbi[:, 0:n], lhsT=ones_b[:], rhs=wrow[:, 512 * i : 512 * i + n], start=True, stop=True
+            )
+            wb.append(wbi)
+        wqk = const.tile([P, 2 * D], F32)
+        nc.vector.tensor_copy(out=wqk[:], in_=wb[3][:, 0 : 2 * D])
+
+        h = const.tile([P, NA, E], BF16)
+        junk = const.tile([P, E], BF16)
+        ssx = const.tile([P, NA], F32)
+        msx = const.tile([P, NA], F32)
+        rx = const.tile([P, NA], F32)
+        h_codes = const.tile([P, NG, S], U32, align_bytes=64)
+        h_scales = const.tile([P, NG, S], U8, align_bytes=64)
+
+        def x_square(a):
+            nc.scalar.activation(
+                out=junk[:], in_=x_sb[:, a, :], func=ACT.Square, accum_out=ssx[:, a : a + 1]
+            )
+            nc.gpsimd.tensor_scalar(
+                out=msx[:, a : a + 1],
+                in0=ssx[:, a : a + 1],
+                scalar1=1.0 / E,
+                scalar2=EPS,
+                op0=ALU.mult,
+                op1=ALU.add,
+            )
+            nc.gpsimd.tensor_tensor(
+                out=rx[:, a : a + 1], in0=msx[:, a : a + 1], in1=neghalf[:], op=ALU.pow
+            )
+
+        def h_make(a):
+            for gu in range(2 * NG):
+                sl = slice(gu * 256, (gu + 1) * 256)
+                wsl = slice((gu % 2) * 256, (gu % 2) * 256 + 256)
+                nc.vector.scalar_tensor_tensor(
+                    out=h[:, a, sl].rearrange("p (e q) -> p e q", e=2),
+                    in0=x_sb[:, a, sl].rearrange("p (q e) -> p e q", e=2),
+                    scalar=rx[:, a : a + 1],
+                    in1=wb[gu // 2][:, wsl].rearrange("p (q e) -> p e q", e=2),
+                    op0=ALU.mult,
+                    op1=ALU.mult,
+                )
+
+        hts = {}
+        hgs = {}
+
+        def h_transpose(pr):
+            for g in range(NG):
+                ht = psum_t.tile([P, 2, 4, P], BF16, tag="tp")
+                for i in range(2):
+                    for t4 in range(4):
+                        lo = (4 * g + t4) * P
+                        nc.tensor.transpose(ht[:, i, t4, :], h[:, 2 * pr + i, lo : lo + P], ident_b[:])
+                hts[(pr, g)] = ht
+
+        def h_copy(pr, g, eng):
+            hg = grp.tile([P, 2, P, 4], BF16, tag="hg", align_bytes=64)
+            src = hts[(pr, g)][:].rearrange("p i t r -> p i r t")
+            if eng == "s":
+                nc.scalar.copy(out=hg[:], in_=src)
+            else:
+                nc.vector.tensor_copy(out=hg[:], in_=src)
+            hgs[(pr, g)] = hg
+
+        def h_quant(pr, g):
+            cols = slice(pr * 256, (pr + 1) * 256)
+            nc.vector.quantize_mx(
+                out=h_codes[:, g, cols].bitcast(FP8X4),
+                scales=h_scales[:, g, cols],
+                in_=hgs[(pr, g)][:].rearrange("p i r t -> p (i r t)"),
+            )
+
+        cos_t = const.tile([P, NA, D], F32)
+        sin_t = const.tile([P, NA, D], F32)
+        tabs = {}
+
+        def sin_tables():
+            pieces = (
+                (cos_t, 0, 0, 48, 0, 24, 2, 1.0),
+                (cos_t, 0, 48, 128, 24, 44, 4, 1.0),
+                (sin_t, 1, 0, 48, 0, 24, 2, -1.0),
+                (sin_t, 1, 48, 64, 24, 40, 1, -1.0),
+                (sin_t, 1, 64, 68, 40, 44, 1, 1.0),
+                (sin_t, 1, 68, 128, 24, 44, 3, 1.0),
+            )
+            for dst, s, d0, d1, j0, j1, r, sign in pieces:
+                nc.scalar.activation(
+                    out=dst[:, :, d0:d1].rearrange("p a (r j) -> p a r j", r=r),
+                    in_=fr[:, s, j0:j1, :]
+                    .rearrange("p j a -> p a j")
+                    .unsqueeze(2)
+                    .to_broadcast([P, NA, r, j1 - j0]),
+                    func=ACT.Sin,
+                    scale=sign * TWO_PI,
+                )
+
+        def w_tables():
+            for i, nm in enumerate(("q", "k")):
+                ta = const.tile([P, NA, D], F32, name="ta_" + nm)
+                tb = const.tile([P, NA, D], F32, name="tb_" + nm)
+                w0 = i * D
+                nc.gpsimd.tensor_tensor(
+                    out=ta[:],
+                    in0=cos_t[:],
+                    in1=wqk[:, w0 : w0 + D].unsqueeze(1).to_broadcast([P, NA, D]),
+                    op=ALU.mult,
+                )
+                nc.gpsimd.tensor_tensor(
+                    out=tb[:, :, 0:64],
+                    in0=sin_t[:, :, 64:128],
+                    in1=wqk[:, w0 : w0 + 64].unsqueeze(1).to_broadcast([P, NA, 64]),
+                    op=ALU.mult,
+                )
+                nc.gpsimd.tensor_tensor(
+                    out=tb[:, :, 64:128],
+                    in0=sin_t[:, :, 0:64],
+                    in1=wqk[:, w0 + 64 : w0 + D].unsqueeze(1).to_broadcast([P, NA, 64]),
+                    op=ALU.mult,
+                )
+                tabs[nm] = (ta, tb)
+
+        wts = {}
+        wgs = {}
+        wcodes = {}
+
+        def w_transpose(unit):
+            c, g, bp = unit // 6, (unit % 6) // 2, unit % 2
+            wt = psum_t.tile([P, 2, 256], F32, tag="tp")
+            for bl in range(2):
+                for u in range(2):
+                    lo = 256 * g + 128 * u
+                    nc.tensor.transpose(
+                        wt[:, u, bl * P : (bl + 1) * P],
+                        raw[c][:, 2 * bp + bl, :].bitcast(F32)[:, lo : lo + P],
+                        ident_f[:],
+                    )
+            wts[unit] = wt
+
+        def w_copy(unit, eng):
+            bp = unit % 2
+            if bp == 0:
+                wg = grp.tile([P, 2048], BF16, tag="wg", align_bytes=64)
+                wgs[unit // 2] = wg
+            wg32 = wgs[unit // 2][:].bitcast(F32).rearrange("p (n u) -> p n u", u=2)
+            dst = wg32[:, bp * 256 : (bp + 1) * 256, :]
+            src = wts[unit][:].rearrange("p u n -> p n u")
+            if eng == "s":
+                nc.scalar.copy(out=dst, in_=src)
+            else:
+                nc.vector.tensor_copy(out=dst, in_=src)
+
+        def w_quant(tile_no):
+            c, g = tile_no // 3, tile_no % 3
+            if g == 0:
+                codes = codep.tile([P, NG, 512], U32, tag="codes", align_bytes=64)
+                scales = codep.tile([P, NG, 512], U8, tag="scales", align_bytes=64)
+                wcodes[c] = (codes, scales)
+            codes, scales = wcodes[c]
+            nc.vector.quantize_mx(
+                out=codes[:, g, :].bitcast(FP8X4), scales=scales[:, g, :], in_=wgs[tile_no][:]
+            )
+
+        accs = {}
+        rss = {}
+        prods = {}
+
+        def mx(slot):
+            c, a = slot // NA, slot % NA
+            codes, scales = wcodes[c]
+            acc = psum_a.tile([P, 512], F32, tag="acc")
+            for g in range(NG):
+                nc.tensor.matmul_mx(
+                    out=acc[:],
+                    lhsT=h_codes[:, g, a * P : (a + 1) * P].bitcast(FP8X4),
+                    lhsT_scale=h_scales[:, g, a * P : (a + 1) * P],
+                    rhs=codes[:, g, :].bitcast(FP8X4),
+                    rhs_scale=scales[:, g, :],
+                    start=(g == 0),
+                    stop=(g == NG - 1),
+                )
+            accs[slot] = acc
+
+        def head_norm(slot):
+            acc = accs[slot]
+            ss = small.tile([P, 4], F32, tag="ss")
+            rs = small.tile([P, 4], F32, tag="rs")
+            for hh in range(4):
+                sq = small.tile([P, D], BF16, tag="sq")
+                nc.scalar.activation(
+                    out=sq[:],
+                    in_=acc[:, hh * D : (hh + 1) * D],
+                    func=ACT.Square,
+                    accum_out=ss[:, hh : hh + 1],
+                )
+            nc.scalar.activation(
+                out=rs[:], in_=ss[:], func=ACT.Abs_reciprocal_sqrt, scale=1.0 / D, bias=eps_t[:]
+            )
+            rss[slot] = rs
+
+        def rope_products(slot):
+            c, a = slot // NA, slot % NA
+            acc = accs[slot]
+            rs = rss[slot]
+            ta, tb = tabs["q" if c < 8 else "k"]
+            t1 = ep.tile([P, 4, D], F32, tag="t1")
+            t2 = ep.tile([P, 4, D], F32, tag="t2")
+            for hh in range(4):
+                for dst, tab in ((t1, ta), (t2, tb)):
+                    nc.vector.scalar_tensor_tensor(
+                        out=dst[:, hh, :],
+                        in0=acc[:, hh * D : (hh + 1) * D],
+                        scalar=rs[:, hh : hh + 1],
+                        in1=tab[:, a, :],
+                        op0=ALU.mult,
+                        op1=ALU.mult,
+                    )
+            prods[slot] = (t1, t2)
+
+        def rope_add_store(slot):
+            c, a = slot // NA, slot % NA
+            t1, t2 = prods[slot]
+            o = outp.tile([P, 4, D], F32, tag="o")
+            nc.gpsimd.tensor_tensor(
+                out=o[:, :, 0:64], in0=t1[:, :, 0:64], in1=t2[:, :, 64:128], op=ALU.add
+            )
+            nc.gpsimd.tensor_tensor(
+                out=o[:, :, 64:128], in0=t1[:, :, 64:128], in1=t2[:, :, 0:64], op=ALU.add
+            )
+            nc.sync.dma_start(out=o_dst(c, a), in_=o[:])
+
+        def v_copy_store(slot, eng):
+            c, a = slot // NA, slot % NA
+            o = outp.tile([P, 4, D], F32, tag="o")
+            if eng == "s":
+                nc.scalar.copy(out=o[:].rearrange("p h d -> p (h d)"), in_=accs[slot][:])
+            else:
+                nc.vector.tensor_copy(out=o[:].rearrange("p h d -> p (h d)"), in_=accs[slot][:])
+            nc.sync.dma_start(out=o_dst(c, a), in_=o[:])
+
+        def t_run(r):
+            for unit in range(3 * r, 3 * r + 3):
+                w_transpose(unit)
+            if r % 2 == 1 and r // 2 + RAW_BUFS < NC:
+                load_w(r // 2 + RAW_BUFS)
+
+        def quants_after_run(r):
+            if r % 2 == 0:
+                w_quant(3 * (r // 2))
+            else:
+                w_quant(3 * (r // 2) + 1)
+                w_quant(3 * (r // 2) + 2)
+
+        for a in range(NA):
+            x_square(a)
+        h_make(0)
+        h_make(1)
+        sin_tables()
+        w_tables()
+        t_run(0)
+        for unit in range(0, 3):
+            w_copy(unit, "s")
+        h_transpose(0)
+        h_make(2)
+        h_make(3)
+        for g in range(NG):
+            h_copy(0, g, "s")
+        quants_after_run(0)
+        for g in range(NG):
+            h_quant(0, g)
+        t_run(1)
+        for unit in range(3, 6):
+            w_copy(unit, "s")
+        h_transpose(1)
+        h_copy(1, 0, "s")
+        h_copy(1, 1, "v")
+        h_copy(1, 2, "v")
+        quants_after_run(1)
+        for g in range(NG):
+            h_quant(1, g)
+        t_run(2)
+        for unit in range(6, 9):
+            w_copy(unit, "s")
+
+        NPAIR = NC * NA // 2
+        for m in range(NPAIR):
+            last = m >= NPAIR - 2
+            mx(2 * m)
+            mx(2 * m + 1)
+            r = m + 3
+            more = r < 2 * NC
+            if more:
+                t_run(r)
+            if m + 2 < 2 * NC:
+                quants_after_run(m + 2)
+            if last:
+                v_copy_store(2 * m, "s")
+                v_copy_store(2 * m + 1, "v")
+            else:
+                head_norm(2 * m)
+                if more:
+                    w_copy(3 * r, "s")
+                rope_products(2 * m)
+                rope_add_store(2 * m)
+                head_norm(2 * m + 1)
+                if more:
+                    w_copy(3 * r + 1, "s")
+                    w_copy(3 * r + 2, "s")
+                rope_products(2 * m + 1)
+                rope_add_store(2 * m + 1)

@@ -56,18 +56,18 @@ def tile_selectivetransformerlayer_pa_kernel(
         o2_v = out_2.rearrange("o h (a p) d -> p (o h) a d", p=P)
 
         def w_src(c):
-            if c < 8:
-                return wq_v[c]
-            if c == 8:
+            if c == 0:
+                return wv_v
+            if c == NC - 1:
                 return wk_v
-            return wv_v
+            return wq_v[c - 1]
 
         def o_dst(c, a):
-            if c < 8:
-                return o0_v[:, 4 * c : 4 * c + 4, a, :]
-            if c == 8:
+            if c == 0:
+                return o2_v[:, :, a, :]
+            if c == NC - 1:
                 return o1_v[:, :, a, :]
-            return o2_v[:, :, a, :]
+            return o0_v[:, 4 * (c - 1) : 4 * c, a, :]
 
         wrow = const.tile([P, E + 2 * D], BF16)
         nc.vector.memset(wrow[:], 0.0)
@@ -346,47 +346,59 @@ def tile_selectivetransformerlayer_pa_kernel(
             c, a = slot // NA, slot % NA
             acc = accs[slot]
             rs = rss[slot]
-            ta, tb = tabs["q" if c < 8 else "k"]
-            t1 = ep.tile([P, 4, D], F32, tag="t1")
-            t2 = ep.tile([P, 4, D], F32, tag="t2")
+            ta, tb = tabs["k" if c == NC - 1 else "q"]
+            if slot % 2 == 0:
+                t1 = ep.tile([P, 2, 4, D], F32, tag="t1")
+                t2 = ep.tile([P, 2, 4, D], F32, tag="t2")
+                prods[slot // 2] = (t1, t2)
+            t1, t2 = prods[slot // 2]
             for hh in range(4):
                 for dst, tab in ((t1, ta), (t2, tb)):
                     nc.vector.scalar_tensor_tensor(
-                        out=dst[:, hh, :],
+                        out=dst[:, slot % 2, hh, :],
                         in0=acc[:, hh * D : (hh + 1) * D],
                         scalar=rs[:, hh : hh + 1],
                         in1=tab[:, a, :],
                         op0=ALU.mult,
                         op1=ALU.mult,
                     )
-            prods[slot] = (t1, t2)
 
-        def rope_add_store(slot):
-            c, a = slot // NA, slot % NA
-            t1, t2 = prods[slot]
-            o = outp.tile([P, 4, D], F32, tag="o")
-            nc.gpsimd.tensor_tensor(
-                out=o[:, :, 0:64], in0=t1[:, :, 0:64], in1=t2[:, :, 64:128], op=ALU.add
-            )
-            nc.gpsimd.tensor_tensor(
-                out=o[:, :, 64:128], in0=t1[:, :, 64:128], in1=t2[:, :, 0:64], op=ALU.add
-            )
-            nc.sync.dma_start(out=o_dst(c, a), in_=o[:])
+        outs = {}
 
-        def v_copy_store(slot, eng):
+        def out_tile(pair):
+            o = outp.tile([P, 2, 4, D], F32, tag="o")
+            outs[pair] = o
+
+        def rope_add(pair, parts):
+            t1, t2 = prods[pair]
+            o = outs[pair]
+            for sl in parts:
+                ov = o[:, sl].rearrange("p i h d -> p (i h) d")
+                v1 = t1[:, sl].rearrange("p i h d -> p (i h) d")
+                v2 = t2[:, sl].rearrange("p i h d -> p (i h) d")
+                nc.gpsimd.tensor_tensor(
+                    out=ov[:, :, 0:64], in0=v1[:, :, 0:64], in1=v2[:, :, 64:128], op=ALU.add
+                )
+                nc.gpsimd.tensor_tensor(
+                    out=ov[:, :, 64:128], in0=v1[:, :, 64:128], in1=v2[:, :, 0:64], op=ALU.add
+                )
+
+        def store(slot):
             c, a = slot // NA, slot % NA
-            o = outp.tile([P, 4, D], F32, tag="o")
+            nc.sync.dma_start(out=o_dst(c, a), in_=outs[slot // 2][:, slot % 2])
+
+        def v_copy(slot, eng):
+            dst = outs[slot // 2][:, slot % 2].rearrange("p h d -> p (h d)")
             if eng == "s":
-                nc.scalar.copy(out=o[:].rearrange("p h d -> p (h d)"), in_=accs[slot][:])
+                nc.scalar.copy(out=dst, in_=accs[slot][:])
             else:
-                nc.vector.tensor_copy(out=o[:].rearrange("p h d -> p (h d)"), in_=accs[slot][:])
-            nc.sync.dma_start(out=o_dst(c, a), in_=o[:])
+                nc.vector.tensor_copy(out=dst, in_=accs[slot][:])
 
-        def t_run(r):
-            for unit in range(3 * r, 3 * r + 3):
+        def t_units(units):
+            for unit in units:
                 w_transpose(unit)
-            if r % 2 == 1 and r // 2 + RAW_BUFS < NC:
-                load_w(r // 2 + RAW_BUFS)
+                if unit % 6 == 5 and unit // 6 + RAW_BUFS < NC:
+                    load_w(unit // 6 + RAW_BUFS)
 
         def quants_after_run(r):
             if r % 2 == 0:
@@ -401,7 +413,7 @@ def tile_selectivetransformerlayer_pa_kernel(
         h_make(1)
         sin_tables()
         w_tables()
-        t_run(0)
+        t_units(range(0, 3))
         for unit in range(0, 3):
             w_copy(unit, "s")
         h_transpose(0)
@@ -412,7 +424,7 @@ def tile_selectivetransformerlayer_pa_kernel(
         quants_after_run(0)
         for g in range(NG):
             h_quant(0, g)
-        t_run(1)
+        t_units(range(3, 6))
         for unit in range(3, 6):
             w_copy(unit, "s")
         h_transpose(1)
@@ -422,33 +434,50 @@ def tile_selectivetransformerlayer_pa_kernel(
         quants_after_run(1)
         for g in range(NG):
             h_quant(1, g)
-        t_run(2)
+        t_units(range(6, 9))
         for unit in range(6, 9):
             w_copy(unit, "s")
 
         NPAIR = NC * NA // 2
+        NRUN = 2 * NC
         for m in range(NPAIR):
-            last = m >= NPAIR - 2
-            mx(2 * m)
-            mx(2 * m + 1)
             r = m + 3
-            more = r < 2 * NC
+            more = r < NRUN
+            mx(2 * m)
             if more:
-                t_run(r)
-            if m + 2 < 2 * NC:
+                t_units((3 * r, 3 * r + 1))
+            mx(2 * m + 1)
+            if more:
+                t_units((3 * r + 2,))
+            if m + 2 < NRUN:
                 quants_after_run(m + 2)
-            if last:
-                v_copy_store(2 * m, "s")
-                v_copy_store(2 * m + 1, "v")
+            out_tile(m)
+            if m < 2:
+                v_copy(2 * m, "s")
+                store(2 * m)
+                if more:
+                    w_copy(3 * r, "s")
+                v_copy(2 * m + 1, "v")
+                store(2 * m + 1)
+                if more:
+                    w_copy(3 * r + 1, "s")
+                    w_copy(3 * r + 2, "s")
             else:
                 head_norm(2 * m)
                 if more:
                     w_copy(3 * r, "s")
                 rope_products(2 * m)
-                rope_add_store(2 * m)
+                if m == NPAIR - 1:
+                    rope_add(m, (slice(0, 1),))
+                    store(2 * m)
                 head_norm(2 * m + 1)
                 if more:
                     w_copy(3 * r + 1, "s")
                     w_copy(3 * r + 2, "s")
                 rope_products(2 * m + 1)
-                rope_add_store(2 * m + 1)
+                if m == NPAIR - 1:
+                    rope_add(m, (slice(1, 2),))
+                else:
+                    rope_add(m, (slice(0, 2),))
+                    store(2 * m)
+                store(2 * m + 1)

@@ -47,13 +47,13 @@ def tile_selectivetransformerlayer_pa_kernel(
         if MANUAL:
             ctx.enter_context(tc.manual_schedule())
 
-        x_v = x.rearrange("o (a p) k -> p (o a) k", p=P)
+        x_v = x.rearrange("o (p a) k -> p (o a) k", a=NA)
         wq_v = wq.rearrange("(c b p) k -> c p b k", b=4, p=P)
         wk_v = wk.rearrange("(b p) k -> p b k", p=P)
         wv_v = wv.rearrange("(b p) k -> p b k", p=P)
-        o0_v = out_0.rearrange("o h (a p) d -> p (o h) a d", p=P)
-        o1_v = out_1.rearrange("o h (a p) d -> p (o h) a d", p=P)
-        o2_v = out_2.rearrange("o h (a p) d -> p (o h) a d", p=P)
+        o0_v = out_0.rearrange("o h (p a) d -> p (o h) (a d)", a=NA)
+        o1_v = out_1.rearrange("o h (p a) d -> p (o h) (a d)", a=NA)
+        o2_v = out_2.rearrange("o h (p a) d -> p (o h) (a d)", a=NA)
 
         def w_src(c):
             if c == 0:
@@ -62,12 +62,13 @@ def tile_selectivetransformerlayer_pa_kernel(
                 return wk_v
             return wq_v[c - 1]
 
-        def o_dst(c, a):
+        def o_dst(c, a0, a1):
+            cols = slice(a0 * D, a1 * D)
             if c == 0:
-                return o2_v[:, :, a, :]
+                return o2_v[:, :, cols]
             if c == NC - 1:
-                return o1_v[:, :, a, :]
-            return o0_v[:, 4 * (c - 1) : 4 * c, a, :]
+                return o1_v[:, :, cols]
+            return o0_v[:, 4 * (c - 1) : 4 * c, cols]
 
         wrow = const.tile([P, E + 2 * D], BF16)
         nc.vector.memset(wrow[:], 0.0)
@@ -98,7 +99,7 @@ def tile_selectivetransformerlayer_pa_kernel(
             load_w(c)
 
         tpos_i = const.tile([P, NA], I32)
-        nc.gpsimd.iota(tpos_i[:], pattern=[[P, NA]], base=0, channel_multiplier=1)
+        nc.gpsimd.iota(tpos_i[:], pattern=[[1, NA]], base=0, channel_multiplier=NA)
         ident_f = const.tile([P, P], F32)
         make_identity(nc, ident_f[:])
         ident_b = const.tile([P, P], BF16)
@@ -325,10 +326,12 @@ def tile_selectivetransformerlayer_pa_kernel(
                 )
             accs[slot] = acc
 
-        def head_norm(slot):
+        sss = {}
+
+        def head_squares(slot):
             acc = accs[slot]
             ss = small.tile([P, 4], F32, tag="ss")
-            rs = small.tile([P, 4], F32, tag="rs")
+            sss[slot] = ss
             for hh in range(4):
                 sq = small.tile([P, D], BF16, tag="sq")
                 nc.scalar.activation(
@@ -337,8 +340,11 @@ def tile_selectivetransformerlayer_pa_kernel(
                     func=ACT.Square,
                     accum_out=ss[:, hh : hh + 1],
                 )
+
+        def head_rsqrt(slot):
+            rs = small.tile([P, 4], F32, tag="rs")
             nc.scalar.activation(
-                out=rs[:], in_=ss[:], func=ACT.Abs_reciprocal_sqrt, scale=1.0 / D, bias=eps_t[:]
+                out=rs[:], in_=sss[slot][:], func=ACT.Abs_reciprocal_sqrt, scale=1.0 / D, bias=eps_t[:]
             )
             rss[slot] = rs
 
@@ -348,14 +354,14 @@ def tile_selectivetransformerlayer_pa_kernel(
             rs = rss[slot]
             ta, tb = tabs["k" if c == NC - 1 else "q"]
             if slot % 2 == 0:
-                t1 = ep.tile([P, 2, 4, D], F32, tag="t1")
-                t2 = ep.tile([P, 2, 4, D], F32, tag="t2")
+                t1 = ep.tile([P, 4, 2, D], F32, tag="t1")
+                t2 = ep.tile([P, 4, 2, D], F32, tag="t2")
                 prods[slot // 2] = (t1, t2)
             t1, t2 = prods[slot // 2]
             for hh in range(4):
                 for dst, tab in ((t1, ta), (t2, tb)):
                     nc.vector.scalar_tensor_tensor(
-                        out=dst[:, slot % 2, hh, :],
+                        out=dst[:, hh, slot % 2, :],
                         in0=acc[:, hh * D : (hh + 1) * D],
                         scalar=rs[:, hh : hh + 1],
                         in1=tab[:, a, :],
@@ -366,33 +372,37 @@ def tile_selectivetransformerlayer_pa_kernel(
         outs = {}
 
         def out_tile(pair):
-            o = outp.tile([P, 2, 4, D], F32, tag="o")
+            o = outp.tile([P, 4, 2, D], F32, tag="o")
             outs[pair] = o
 
-        def rope_add(pair, parts):
+        def rope_add(pair, i0, i1):
             t1, t2 = prods[pair]
             o = outs[pair]
-            for sl in parts:
-                ov = o[:, sl].rearrange("p i h d -> p (i h) d")
-                v1 = t1[:, sl].rearrange("p i h d -> p (i h) d")
-                v2 = t2[:, sl].rearrange("p i h d -> p (i h) d")
-                nc.gpsimd.tensor_tensor(
-                    out=ov[:, :, 0:64], in0=v1[:, :, 0:64], in1=v2[:, :, 64:128], op=ALU.add
-                )
-                nc.gpsimd.tensor_tensor(
-                    out=ov[:, :, 64:128], in0=v1[:, :, 64:128], in1=v2[:, :, 0:64], op=ALU.add
-                )
+            ov = o[:, :, i0:i1, :].rearrange("p h i d -> p (h i) d") if i1 - i0 == 2 else o[:, :, i0, :]
+            v1 = t1[:, :, i0:i1, :].rearrange("p h i d -> p (h i) d") if i1 - i0 == 2 else t1[:, :, i0, :]
+            v2 = t2[:, :, i0:i1, :].rearrange("p h i d -> p (h i) d") if i1 - i0 == 2 else t2[:, :, i0, :]
+            nc.gpsimd.tensor_tensor(
+                out=ov[:, :, 0:64], in0=v1[:, :, 0:64], in1=v2[:, :, 64:128], op=ALU.add
+            )
+            nc.gpsimd.tensor_tensor(
+                out=ov[:, :, 64:128], in0=v1[:, :, 64:128], in1=v2[:, :, 0:64], op=ALU.add
+            )
 
-        def store(slot):
-            c, a = slot // NA, slot % NA
-            nc.sync.dma_start(out=o_dst(c, a), in_=outs[slot // 2][:, slot % 2])
+        def store(pair, i0, i1):
+            c, a = (2 * pair) // NA, (2 * pair) % NA
+            src = outs[pair]
+            if i1 - i0 == 2:
+                nc.sync.dma_start(out=o_dst(c, a, a + 2), in_=src[:].rearrange("p h i d -> p h (i d)"))
+            else:
+                nc.sync.dma_start(out=o_dst(c, a + i0, a + i1), in_=src[:, :, i0, :])
 
         def v_copy(slot, eng):
-            dst = outs[slot // 2][:, slot % 2].rearrange("p h d -> p (h d)")
+            dst = outs[slot // 2][:, :, slot % 2, :]
+            src = accs[slot][:].rearrange("p (h d) -> p h d", d=D)
             if eng == "s":
-                nc.scalar.copy(out=dst, in_=accs[slot][:])
+                nc.scalar.copy(out=dst, in_=src)
             else:
-                nc.vector.tensor_copy(out=dst, in_=accs[slot][:])
+                nc.vector.tensor_copy(out=dst, in_=src)
 
         def t_units(units):
             for unit in units:
@@ -454,30 +464,36 @@ def tile_selectivetransformerlayer_pa_kernel(
             out_tile(m)
             if m < 2:
                 v_copy(2 * m, "s")
-                store(2 * m)
-                if more:
-                    w_copy(3 * r, "s")
+                w_copy(3 * r, "s")
                 v_copy(2 * m + 1, "v")
-                store(2 * m + 1)
-                if more:
-                    w_copy(3 * r + 1, "s")
-                    w_copy(3 * r + 2, "s")
+                store(m, 0, 2)
+                w_copy(3 * r + 1, "s")
+                w_copy(3 * r + 2, "s")
+            elif more:
+                head_squares(2 * m)
+                w_copy(3 * r, "s")
+                head_rsqrt(2 * m)
+                rope_products(2 * m)
+                head_squares(2 * m + 1)
+                w_copy(3 * r + 1, "s")
+                head_rsqrt(2 * m + 1)
+                w_copy(3 * r + 2, "s")
+                rope_products(2 * m + 1)
+                rope_add(m, 0, 2)
+                store(m, 0, 2)
             else:
-                head_norm(2 * m)
-                if more:
-                    w_copy(3 * r, "s")
+                head_squares(2 * m)
+                head_squares(2 * m + 1)
+                head_rsqrt(2 * m)
+                head_rsqrt(2 * m + 1)
                 rope_products(2 * m)
                 if m == NPAIR - 1:
-                    rope_add(m, (slice(0, 1),))
-                    store(2 * m)
-                head_norm(2 * m + 1)
-                if more:
-                    w_copy(3 * r + 1, "s")
-                    w_copy(3 * r + 2, "s")
+                    rope_add(m, 0, 1)
+                    store(m, 0, 1)
                 rope_products(2 * m + 1)
                 if m == NPAIR - 1:
-                    rope_add(m, (slice(1, 2),))
+                    rope_add(m, 1, 2)
+                    store(m, 1, 2)
                 else:
-                    rope_add(m, (slice(0, 2),))
-                    store(2 * m)
-                store(2 * m + 1)
+                    rope_add(m, 0, 2)
+                    store(m, 0, 2)

@@ -56,19 +56,19 @@ def tile_selectivetransformerlayer_pa_kernel(
         o2_v = out_2.rearrange("o h (p a) d -> p (o h) (a d)", a=NA)
 
         def w_src(c):
-            if c == 0:
-                return wv_v
             if c == NC - 1:
+                return wv_v
+            if c == NC - 2:
                 return wk_v
-            return wq_v[c - 1]
+            return wq_v[c]
 
         def o_dst(c, a0, a1):
             cols = slice(a0 * D, a1 * D)
-            if c == 0:
-                return o2_v[:, :, cols]
             if c == NC - 1:
+                return o2_v[:, :, cols]
+            if c == NC - 2:
                 return o1_v[:, :, cols]
-            return o0_v[:, 4 * (c - 1) : 4 * c, cols]
+            return o0_v[:, 4 * c : 4 * c + 4, cols]
 
         wrow = const.tile([P, E + 2 * D], BF16)
         nc.vector.memset(wrow[:], 0.0)
@@ -81,11 +81,13 @@ def tile_selectivetransformerlayer_pa_kernel(
         neghalf = const.tile([P, 1], F32)
         nc.vector.memset(neghalf[:], -0.5)
 
+        x_sb = const.tile([P, NA, E], BF16)
+        for a in range(2):
+            nc.sync.dma_start(out=x_sb[:, a, :], in_=x_v[:, a, :])
         nc.sync.dma_start(out=wrow[0:1, 0:E], in_=ln1_w.unsqueeze(0))
         nc.sync.dma_start(out=wrow[0:1, E : E + D], in_=q_norm_w.unsqueeze(0))
         nc.sync.dma_start(out=wrow[0:1, E + D : E + 2 * D], in_=k_norm_w.unsqueeze(0))
-        x_sb = const.tile([P, NA, E], BF16)
-        for a in range(NA):
+        for a in range(2, NA):
             nc.sync.dma_start(out=x_sb[:, a, :], in_=x_v[:, a, :])
 
         raw = {}
@@ -242,11 +244,12 @@ def tile_selectivetransformerlayer_pa_kernel(
 
         def w_tables():
             for i, nm in enumerate(("q", "k")):
-                ta = const.tile([P, NA, D], F32, name="ta_" + nm)
-                tb = const.tile([P, NA, D], F32, name="tb_" + nm)
+                tab = const.tile([P, NA, 2, D], F32, name="tab_" + nm)
+                ta = tab[:, :, 0, :]
+                tb = tab[:, :, 1, :]
                 w0 = i * D
                 nc.gpsimd.tensor_tensor(
-                    out=ta[:],
+                    out=ta,
                     in0=cos_t[:],
                     in1=wqk[:, w0 : w0 + D].unsqueeze(1).to_broadcast([P, NA, D]),
                     op=ALU.mult,
@@ -263,7 +266,7 @@ def tile_selectivetransformerlayer_pa_kernel(
                     in1=wqk[:, w0 + 64 : w0 + D].unsqueeze(1).to_broadcast([P, NA, 64]),
                     op=ALU.mult,
                 )
-                tabs[nm] = (ta, tb)
+                tabs[nm] = tab
 
         wts = {}
         wgs = {}
@@ -352,22 +355,20 @@ def tile_selectivetransformerlayer_pa_kernel(
             c, a = slot // NA, slot % NA
             acc = accs[slot]
             rs = rss[slot]
-            ta, tb = tabs["k" if c == NC - 1 else "q"]
+            tab = tabs["k" if c == NC - 2 else "q"]
             if slot % 2 == 0:
-                t1 = ep.tile([P, 4, 2, D], F32, tag="t1")
-                t2 = ep.tile([P, 4, 2, D], F32, tag="t2")
-                prods[slot // 2] = (t1, t2)
-            t1, t2 = prods[slot // 2]
+                t12 = ep.tile([P, 4, 2, 2, D], F32, tag="t12")
+                prods[slot // 2] = t12
+            t12 = prods[slot // 2]
             for hh in range(4):
-                for dst, tab in ((t1, ta), (t2, tb)):
-                    nc.vector.scalar_tensor_tensor(
-                        out=dst[:, hh, slot % 2, :],
-                        in0=acc[:, hh * D : (hh + 1) * D],
-                        scalar=rs[:, hh : hh + 1],
-                        in1=tab[:, a, :],
-                        op0=ALU.mult,
-                        op1=ALU.mult,
-                    )
+                nc.vector.scalar_tensor_tensor(
+                    out=t12[:, hh, slot % 2, :, :],
+                    in0=acc[:, hh * D : (hh + 1) * D].unsqueeze(1).to_broadcast([P, 2, D]),
+                    scalar=rs[:, hh : hh + 1],
+                    in1=tab[:, a, :, :],
+                    op0=ALU.mult,
+                    op1=ALU.mult,
+                )
 
         outs = {}
 
@@ -375,17 +376,20 @@ def tile_selectivetransformerlayer_pa_kernel(
             o = outp.tile([P, 4, 2, D], F32, tag="o")
             outs[pair] = o
 
-        def rope_add(pair, i0, i1):
-            t1, t2 = prods[pair]
+        def rope_add(pair, i0, i1, eng):
+            t12 = prods[pair]
             o = outs[pair]
-            ov = o[:, :, i0:i1, :].rearrange("p h i d -> p (h i) d") if i1 - i0 == 2 else o[:, :, i0, :]
-            v1 = t1[:, :, i0:i1, :].rearrange("p h i d -> p (h i) d") if i1 - i0 == 2 else t1[:, :, i0, :]
-            v2 = t2[:, :, i0:i1, :].rearrange("p h i d -> p (h i) d") if i1 - i0 == 2 else t2[:, :, i0, :]
-            nc.gpsimd.tensor_tensor(
-                out=ov[:, :, 0:64], in0=v1[:, :, 0:64], in1=v2[:, :, 64:128], op=ALU.add
+            eng.tensor_tensor(
+                out=o[:, :, i0:i1, 0:64],
+                in0=t12[:, :, i0:i1, 0, 0:64],
+                in1=t12[:, :, i0:i1, 1, 64:128],
+                op=ALU.add,
             )
-            nc.gpsimd.tensor_tensor(
-                out=ov[:, :, 64:128], in0=v1[:, :, 64:128], in1=v2[:, :, 0:64], op=ALU.add
+            eng.tensor_tensor(
+                out=o[:, :, i0:i1, 64:128],
+                in0=t12[:, :, i0:i1, 0, 64:128],
+                in1=t12[:, :, i0:i1, 1, 0:64],
+                op=ALU.add,
             )
 
         def store(pair, i0, i1):
@@ -417,6 +421,9 @@ def tile_selectivetransformerlayer_pa_kernel(
                 w_quant(3 * (r // 2) + 1)
                 w_quant(3 * (r // 2) + 2)
 
+        def preload_rsqrt():
+            nc.scalar.activation(out=warm2[:], in_=eps_t[:], func=ACT.Abs_reciprocal_sqrt)
+
         for a in range(NA):
             x_square(a)
         h_make(0)
@@ -437,63 +444,76 @@ def tile_selectivetransformerlayer_pa_kernel(
         t_units(range(3, 6))
         for unit in range(3, 6):
             w_copy(unit, "s")
-        h_transpose(1)
-        h_copy(1, 0, "s")
-        h_copy(1, 1, "v")
-        h_copy(1, 2, "v")
         quants_after_run(1)
+        preload_rsqrt()
+        h_transpose(1)
+        mx(0)
+        mx(1)
+        for g in range(NG):
+            h_copy(1, g, "v")
         for g in range(NG):
             h_quant(1, g)
         t_units(range(6, 9))
-        for unit in range(6, 9):
-            w_copy(unit, "s")
 
         NPAIR = NC * NA // 2
         NRUN = 2 * NC
-        for m in range(NPAIR):
+        for m in range(NRUN - 3):
             r = m + 3
-            more = r < NRUN
-            mx(2 * m)
-            if more:
-                t_units((3 * r, 3 * r + 1))
-            mx(2 * m + 1)
-            if more:
-                t_units((3 * r + 2,))
-            if m + 2 < NRUN:
-                quants_after_run(m + 2)
             out_tile(m)
-            if m < 2:
-                v_copy(2 * m, "s")
-                w_copy(3 * r, "s")
-                v_copy(2 * m + 1, "v")
-                store(m, 0, 2)
-                w_copy(3 * r + 1, "s")
-                w_copy(3 * r + 2, "s")
-            elif more:
-                head_squares(2 * m)
-                w_copy(3 * r, "s")
-                head_rsqrt(2 * m)
-                rope_products(2 * m)
-                head_squares(2 * m + 1)
-                w_copy(3 * r + 1, "s")
-                head_rsqrt(2 * m + 1)
-                w_copy(3 * r + 2, "s")
-                rope_products(2 * m + 1)
-                rope_add(m, 0, 2)
-                store(m, 0, 2)
+            if m == 0:
+                head_squares(0)
+                head_squares(1)
+                head_rsqrt(0)
+                head_rsqrt(1)
+                for unit in range(6, 9):
+                    w_copy(unit, "s")
+                t_units(range(9, 12))
+                for unit in range(9, 12):
+                    w_copy(unit, "s")
+                rope_products(0)
+                rope_products(1)
+                quants_after_run(2)
             else:
+                mx(2 * m)
+                t_units((3 * r, 3 * r + 1))
+                mx(2 * m + 1)
+                t_units((3 * r + 2,))
+                quants_after_run(m + 2)
                 head_squares(2 * m)
-                head_squares(2 * m + 1)
+                w_copy(3 * r, "s")
                 head_rsqrt(2 * m)
-                head_rsqrt(2 * m + 1)
                 rope_products(2 * m)
-                if m == NPAIR - 1:
-                    rope_add(m, 0, 1)
-                    store(m, 0, 1)
+                head_squares(2 * m + 1)
+                w_copy(3 * r + 1, "s")
+                head_rsqrt(2 * m + 1)
+                w_copy(3 * r + 2, "s")
                 rope_products(2 * m + 1)
-                if m == NPAIR - 1:
-                    rope_add(m, 1, 2)
-                    store(m, 1, 2)
-                else:
-                    rope_add(m, 0, 2)
-                    store(m, 0, 2)
+            rope_add(m, 0, 2, nc.gpsimd)
+            store(m, 0, 2)
+
+        m = NRUN - 3
+        mx(2 * m)
+        mx(2 * m + 1)
+        quants_after_run(NRUN - 1)
+        mx(2 * m + 2)
+        mx(2 * m + 3)
+        for pair in (m, m + 1, m + 2):
+            out_tile(pair)
+        head_squares(2 * m)
+        head_squares(2 * m + 1)
+        head_rsqrt(2 * m)
+        head_rsqrt(2 * m + 1)
+        rope_products(2 * m)
+        rope_add(m, 0, 1, nc.vector)
+        store(m, 0, 1)
+        v_copy(2 * m + 2, "s")
+        v_copy(2 * m + 3, "s")
+        store(m + 1, 0, 2)
+        mx(2 * m + 4)
+        mx(2 * m + 5)
+        rope_products(2 * m + 1)
+        rope_add(m, 1, 2, nc.vector)
+        store(m, 1, 2)
+        v_copy(2 * m + 4, "s")
+        v_copy(2 * m + 5, "s")
+        store(m + 2, 0, 2)

@@ -421,6 +421,10 @@ def tile_selectivetransformerlayer_pa_kernel(
                 w_quant(3 * (r // 2) + 1)
                 w_quant(3 * (r // 2) + 2)
 
+        def warm_pe(n):
+            for i in range(n):
+                nc.tensor.matmul(out=wb[3][:], lhsT=ones_b[:], rhs=wrow[:, 0:512], start=True, stop=True)
+
         def preload_rsqrt():
             nc.scalar.activation(out=warm2[:], in_=eps_t[:], func=ACT.Abs_reciprocal_sqrt)
 
@@ -430,10 +434,13 @@ def tile_selectivetransformerlayer_pa_kernel(
         h_make(1)
         sin_tables()
         w_tables()
+        warm_pe(5)
         t_units(range(0, 3))
+        warm_pe(3)
         for unit in range(0, 3):
             w_copy(unit, "s")
         h_transpose(0)
+        warm_pe(3)
         h_make(2)
         h_make(3)
         for g in range(NG):
@@ -442,6 +449,7 @@ def tile_selectivetransformerlayer_pa_kernel(
         for g in range(NG):
             h_quant(0, g)
         t_units(range(3, 6))
+        warm_pe(3)
         for unit in range(3, 6):
             w_copy(unit, "s")
         quants_after_run(1)
@@ -457,6 +465,7 @@ def tile_selectivetransformerlayer_pa_kernel(
 
         NPAIR = NC * NA // 2
         NRUN = 2 * NC
+        SPLIT_FROM = NRUN - 4
         for m in range(NRUN - 3):
             r = m + 3
             out_tile(m)
@@ -471,30 +480,40 @@ def tile_selectivetransformerlayer_pa_kernel(
                 for unit in range(9, 12):
                     w_copy(unit, "s")
                 rope_products(0)
+                w_quant(3)
                 rope_products(1)
-                quants_after_run(2)
+                w_quant(4)
+                w_quant(5)
             else:
                 mx(2 * m)
                 t_units((3 * r, 3 * r + 1))
                 mx(2 * m + 1)
                 t_units((3 * r + 2,))
-                quants_after_run(m + 2)
                 head_squares(2 * m)
                 w_copy(3 * r, "s")
                 head_rsqrt(2 * m)
                 rope_products(2 * m)
+                if m >= SPLIT_FROM:
+                    rope_add(m, 0, 1, nc.gpsimd)
+                    store(m, 0, 1)
+                if r % 2 == 1:
+                    w_quant(3 * (r // 2) + 1)
                 head_squares(2 * m + 1)
                 w_copy(3 * r + 1, "s")
                 head_rsqrt(2 * m + 1)
                 w_copy(3 * r + 2, "s")
                 rope_products(2 * m + 1)
-            rope_add(m, 0, 2, nc.gpsimd)
-            store(m, 0, 2)
+                w_quant(3 * (r // 2) + (2 if r % 2 == 1 else 0))
+            if m >= SPLIT_FROM:
+                rope_add(m, 1, 2, nc.gpsimd)
+                store(m, 1, 2)
+            else:
+                rope_add(m, 0, 2, nc.gpsimd)
+                store(m, 0, 2)
 
         m = NRUN - 3
         mx(2 * m)
         mx(2 * m + 1)
-        quants_after_run(NRUN - 1)
         mx(2 * m + 2)
         mx(2 * m + 3)
         for pair in (m, m + 1, m + 2):

@@ -421,10 +421,6 @@ def tile_selectivetransformerlayer_pa_kernel(
                 w_quant(3 * (r // 2) + 1)
                 w_quant(3 * (r // 2) + 2)
 
-        def warm_pe(n):
-            for i in range(n):
-                nc.tensor.matmul(out=wb[3][:], lhsT=ones_b[:], rhs=wrow[:, 0:512], start=True, stop=True)
-
         def preload_rsqrt():
             nc.scalar.activation(out=warm2[:], in_=eps_t[:], func=ACT.Abs_reciprocal_sqrt)
 
@@ -434,13 +430,10 @@ def tile_selectivetransformerlayer_pa_kernel(
         h_make(1)
         sin_tables()
         w_tables()
-        warm_pe(5)
         t_units(range(0, 3))
-        warm_pe(3)
         for unit in range(0, 3):
             w_copy(unit, "s")
         h_transpose(0)
-        warm_pe(3)
         h_make(2)
         h_make(3)
         for g in range(NG):
@@ -449,7 +442,6 @@ def tile_selectivetransformerlayer_pa_kernel(
         for g in range(NG):
             h_quant(0, g)
         t_units(range(3, 6))
-        warm_pe(3)
         for unit in range(3, 6):
             w_copy(unit, "s")
         quants_after_run(1)

@@ -26,6 +26,7 @@ EPS = 1e-6
 TWO_PI = 2.0 * math.pi
 RAW_BUFS = 5
 MANUAL = True
+V_COPY_EVERY = 4
 
 FLOPS = 2 * S * E * (NC * 512)
 
@@ -421,6 +422,10 @@ def tile_selectivetransformerlayer_pa_kernel(
                 w_quant(3 * (r // 2) + 1)
                 w_quant(3 * (r // 2) + 2)
 
+        def warm_pe(n):
+            for i in range(n):
+                nc.tensor.matmul(out=wb[3][:], lhsT=ones_b[:], rhs=wrow[:, 0:512], start=True, stop=True)
+
         def preload_rsqrt():
             nc.scalar.activation(out=warm2[:], in_=eps_t[:], func=ACT.Abs_reciprocal_sqrt)
 
@@ -430,10 +435,13 @@ def tile_selectivetransformerlayer_pa_kernel(
         h_make(1)
         sin_tables()
         w_tables()
+        warm_pe(5)
         t_units(range(0, 3))
+        warm_pe(3)
         for unit in range(0, 3):
             w_copy(unit, "s")
         h_transpose(0)
+        warm_pe(3)
         h_make(2)
         h_make(3)
         for g in range(NG):
@@ -442,6 +450,7 @@ def tile_selectivetransformerlayer_pa_kernel(
         for g in range(NG):
             h_quant(0, g)
         t_units(range(3, 6))
+        warm_pe(3)
         for unit in range(3, 6):
             w_copy(unit, "s")
         quants_after_run(1)
@@ -493,7 +502,7 @@ def tile_selectivetransformerlayer_pa_kernel(
                 head_squares(2 * m + 1)
                 w_copy(3 * r + 1, "s")
                 head_rsqrt(2 * m + 1)
-                w_copy(3 * r + 2, "s")
+                w_copy(3 * r + 2, "v" if m % V_COPY_EVERY == 1 else "s")
                 rope_products(2 * m + 1)
                 w_quant(3 * (r // 2) + (2 if r % 2 == 1 else 0))
             if m >= SPLIT_FROM:

@@ -26,7 +26,6 @@ EPS = 1e-6
 TWO_PI = 2.0 * math.pi
 RAW_BUFS = 5
 MANUAL = True
-V_COPY_EVERY = 4
 
 FLOPS = 2 * S * E * (NC * 512)
 
@@ -380,6 +379,15 @@ def tile_selectivetransformerlayer_pa_kernel(
         def rope_add(pair, i0, i1, eng):
             t12 = prods[pair]
             o = outs[pair]
+            if i1 - i0 == 2:
+                split = "p h i (f d) -> p (h i) f d"
+                eng.tensor_tensor(
+                    out=o[:].rearrange(split, f=2),
+                    in0=t12[:, :, :, 0, :].rearrange(split, f=2),
+                    in1=t12[:, :, :, 1, :].rearrange(split, f=2)[:, :, ::-1, :],
+                    op=ALU.add,
+                )
+                return
             eng.tensor_tensor(
                 out=o[:, :, i0:i1, 0:64],
                 in0=t12[:, :, i0:i1, 0, 0:64],
@@ -502,7 +510,7 @@ def tile_selectivetransformerlayer_pa_kernel(
                 head_squares(2 * m + 1)
                 w_copy(3 * r + 1, "s")
                 head_rsqrt(2 * m + 1)
-                w_copy(3 * r + 2, "v" if m % V_COPY_EVERY == 1 else "s")
+                w_copy(3 * r + 2, "s")
                 rope_products(2 * m + 1)
                 w_quant(3 * (r // 2) + (2 if r % 2 == 1 else 0))
             if m >= SPLIT_FROM:

import math
from contextlib import ExitStack

import concourse.mybir as mybir
from concourse.masks import make_identity

F32 = mybir.dt.float32
BF16 = mybir.dt.bfloat16
I32 = mybir.dt.int32
U32 = mybir.dt.uint32
U8 = mybir.dt.uint8
FP8X4 = mybir.dt.float8_e4m3fn_x4
ACT = mybir.ActivationFunctionType
ALU = mybir.AluOpType

P = 128
S = 512
E = 1536
D = 128
NA = S // P
NG = E // 512
NC = 10
NF = 44
ROPE_BASE = 1000000.0
EPS = 1e-6
TWO_PI = 2.0 * math.pi
RAW_BUFS = 5
MANUAL = True

FLOPS = 2 * S * E * (NC * 512)


def tile_selectivetransformerlayer_pa_kernel(
    tc, x, ln1_w, wq, wk, wv, q_norm_w, k_norm_w, out_0, out_1, out_2
):
    nc = tc.nc
    with ExitStack() as ctx:
        const = ctx.enter_context(tc.tile_pool(name="const", bufs=1))
        rawp = ctx.enter_context(tc.tile_pool(name="rawp", bufs=RAW_BUFS))
        codep = ctx.enter_context(tc.tile_pool(name="codep", bufs=3))
        grp = ctx.enter_context(tc.tile_pool(name="grp", bufs=3))
        small = ctx.enter_context(tc.tile_pool(name="small", bufs=4))
        ep = ctx.enter_context(tc.tile_pool(name="ep", bufs=3))
        outp = ctx.enter_context(tc.tile_pool(name="outp", bufs=4))
        psum_t = ctx.enter_context(tc.psum_pool(name="psum_t", bufs=4))
        psum_a = ctx.enter_context(tc.psum_pool(name="psum_a", bufs=4))
        if MANUAL:
            ctx.enter_context(tc.manual_schedule())

        x_v = x.rearrange("o (p a) k -> p (o a) k", a=NA)
        wq_v = wq.rearrange("(c b p) k -> c p b k", b=4, p=P)
        wk_v = wk.rearrange("(b p) k -> p b k", p=P)
        wv_v = wv.rearrange("(b p) k -> p b k", p=P)
        o0_v = out_0.rearrange("o h (p a) d -> p (o h) (a d)", a=NA)
        o1_v = out_1.rearrange("o h (p a) d -> p (o h) (a d)", a=NA)
        o2_v = out_2.rearrange("o h (p a) d -> p (o h) (a d)", a=NA)

        def w_src(c):
            if c == NC - 1:
                return wv_v
            if c == NC - 2:
                return wk_v
            return wq_v[c]

        def o_dst(c, a0, a1):
            cols = slice(a0 * D, a1 * D)
            if c == NC - 1:
                return o2_v[:, :, cols]
            if c == NC - 2:
                return o1_v[:, :, cols]
            return o0_v[:, 4 * c : 4 * c + 4, cols]

        wrow = const.tile([P, E + 2 * D], BF16)
        nc.vector.memset(wrow[:], 0.0)
        ones_b = const.tile([P, P], BF16)
        nc.vector.memset(ones_b[:], 1.0)
        warm = const.tile([P, 1], F32)
        nc.vector.memset(warm[:], 0.0)
        eps_t = const.tile([P, 1], F32)
        nc.vector.memset(eps_t[:], EPS)
        neghalf = const.tile([P, 1], F32)
        nc.vector.memset(neghalf[:], -0.5)

        x_sb = const.tile([P, NA, E], BF16)
        for a in range(2):
            nc.sync.dma_start(out=x_sb[:, a, :], in_=x_v[:, a, :])
        nc.sync.dma_start(out=wrow[0:1, 0:E], in_=ln1_w.unsqueeze(0))
        nc.sync.dma_start(out=wrow[0:1, E : E + D], in_=q_norm_w.unsqueeze(0))
        nc.sync.dma_start(out=wrow[0:1, E + D : E + 2 * D], in_=k_norm_w.unsqueeze(0))
        for a in range(2, NA):
            nc.sync.dma_start(out=x_sb[:, a, :], in_=x_v[:, a, :])

        raw = {}

        def load_w(c):
            w_raw = rawp.tile([P, 4, E], BF16, tag="w_raw")
            nc.sync.dma_start(out=w_raw[:], in_=w_src(c))
            raw[c] = w_raw

        for c in range(RAW_BUFS):
            load_w(c)

        tpos_i = const.tile([P, NA], I32)
        nc.gpsimd.iota(tpos_i[:], pattern=[[1, NA]], base=0, channel_multiplier=NA)
        ident_f = const.tile([P, P], F32)
        make_identity(nc, ident_f[:])
        ident_b = const.tile([P, P], BF16)
        make_identity(nc, ident_b[:])
        warm2 = const.tile([P, 1], F32)
        nc.scalar.activation(out=warm2[:], in_=warm[:], func=ACT.Sin)

        tpos = const.tile([P, NA], F32)
        nc.vector.tensor_copy(out=tpos[:], in_=tpos_i[:])
        turns = const.tile([P, 2, NF, NA], F32)
        for j in range(NF):
            if j < 24:
                cj = ROPE_BASE ** (-2.0 * j / 48.0) / TWO_PI
            else:
                cj = ROPE_BASE ** (-2.0 * (j - 24) / 40.0) / TWO_PI
            nc.vector.tensor_scalar_mul(out=turns[:, 1, j, :], in0=tpos[:], scalar1=cj)
        nc.vector.tensor_scalar_add(out=turns[:, 0], in0=turns[:, 1], scalar1=0.25)
        NT = 2 * NF * NA
        turns_f = turns[:].rearrange("p s j a -> p (s j a)")
        whole_i = const.tile([P, NT], I32)
        nc.vector.tensor_copy(out=whole_i[:], in_=turns_f)
        whole = const.tile([P, NT], F32)
        nc.vector.tensor_copy(out=whole[:], in_=whole_i[:])
        frac = const.tile([P, NT], F32)
        nc.vector.tensor_tensor(out=frac[:], in0=turns_f, in1=whole[:], op=ALU.subtract)
        fneg = const.tile([P, NT], F32)
        nc.vector.scalar_tensor_tensor(
            out=fneg[:], in0=frac[:], scalar=0.5, in1=frac[:], op0=ALU.is_gt, op1=ALU.subtract
        )
        fr = const.tile([P, 2, NF, NA], F32)
        nc.vector.scalar_tensor_tensor(
            out=fr[:].rearrange("p s j a -> p (s j a)"),
            in0=fneg[:],
            scalar=0.5,
            in1=fneg[:],
            op0=ALU.is_gt,
            op1=ALU.subtract,
        )

        wb = []
        for i in range(4):
            n = 512 if i < 3 else 2 * D
            wbi = psum_a.tile([P, 512], F32, tag="acc", name="wb%d" % i)
            nc.tensor.matmul(
                out=wbi[:, 0:n], lhsT=ones_b[:], rhs=wrow[:, 512 * i : 512 * i + n], start=True, stop=True
            )
            wb.append(wbi)
        wqk = const.tile([P, 2 * D], F32)
        nc.vector.tensor_copy(out=wqk[:], in_=wb[3][:, 0 : 2 * D])

        h = const.tile([P, NA, E], BF16)
        junk = const.tile([P, E], BF16)
        ssx = const.tile([P, NA], F32)
        msx = const.tile([P, NA], F32)
        rx = const.tile([P, NA], F32)
        h_codes = const.tile([P, NG, S], U32, align_bytes=64)
        h_scales = const.tile([P, NG, S], U8, align_bytes=64)

        def x_square(a):
            nc.scalar.activation(
                out=junk[:], in_=x_sb[:, a, :], func=ACT.Square, accum_out=ssx[:, a : a + 1]
            )
            nc.gpsimd.tensor_scalar(
                out=msx[:, a : a + 1],
                in0=ssx[:, a : a + 1],
                scalar1=1.0 / E,
                scalar2=EPS,
                op0=ALU.mult,
                op1=ALU.add,
            )
            nc.gpsimd.tensor_tensor(
                out=rx[:, a : a + 1], in0=msx[:, a : a + 1], in1=neghalf[:], op=ALU.pow
            )

        def h_make(a):
            for gu in range(2 * NG):
                sl = slice(gu * 256, (gu + 1) * 256)
                wsl = slice((gu % 2) * 256, (gu % 2) * 256 + 256)
                nc.vector.scalar_tensor_tensor(
                    out=h[:, a, sl].rearrange("p (e q) -> p e q", e=2),
                    in0=x_sb[:, a, sl].rearrange("p (q e) -> p e q", e=2),
                    scalar=rx[:, a : a + 1],
                    in1=wb[gu // 2][:, wsl].rearrange("p (q e) -> p e q", e=2),
                    op0=ALU.mult,
                    op1=ALU.mult,
                )

        hts = {}
        hgs = {}

        def h_transpose(pr):
            for g in range(NG):
                ht = psum_t.tile([P, 2, 4, P], BF16, tag="tp")
                for i in range(2):
                    for t4 in range(4):
                        lo = (4 * g + t4) * P
                        nc.tensor.transpose(ht[:, i, t4, :], h[:, 2 * pr + i, lo : lo + P], ident_b[:])
                hts[(pr, g)] = ht

        def h_copy(pr, g, eng):
            hg = grp.tile([P, 2, P, 4], BF16, tag="hg", align_bytes=64)
            src = hts[(pr, g)][:].rearrange("p i t r -> p i r t")
            if eng == "s":
                nc.scalar.copy(out=hg[:], in_=src)
            else:
                nc.vector.tensor_copy(out=hg[:], in_=src)
            hgs[(pr, g)] = hg

        def h_quant(pr, g):
            cols = slice(pr * 256, (pr + 1) * 256)
            nc.vector.quantize_mx(
                out=h_codes[:, g, cols].bitcast(FP8X4),
                scales=h_scales[:, g, cols],
                in_=hgs[(pr, g)][:].rearrange("p i r t -> p (i r t)"),
            )

        cos_t = const.tile([P, NA, D], F32)
        sin_t = const.tile([P, NA, D], F32)
        tabs = {}

        def sin_tables():
            pieces = (
                (cos_t, 0, 0, 48, 0, 24, 2, 1.0),
                (cos_t, 0, 48, 128, 24, 44, 4, 1.0),
                (sin_t, 1, 0, 48, 0, 24, 2, -1.0),
                (sin_t, 1, 48, 64, 24, 40, 1, -1.0),
                (sin_t, 1, 64, 68, 40, 44, 1, 1.0),
                (sin_t, 1, 68, 128, 24, 44, 3, 1.0),
            )
            for dst, s, d0, d1, j0, j1, r, sign in pieces:
                nc.scalar.activation(
                    out=dst[:, :, d0:d1].rearrange("p a (r j) -> p a r j", r=r),
                    in_=fr[:, s, j0:j1, :]
                    .rearrange("p j a -> p a j")
                    .unsqueeze(2)
                    .to_broadcast([P, NA, r, j1 - j0]),
                    func=ACT.Sin,
                    scale=sign * TWO_PI,
                )

        def w_tables():
            for i, nm in enumerate(("q", "k")):
                tab = const.tile([P, NA, 2, D], F32, name="tab_" + nm)
                ta = tab[:, :, 0, :]
                tb = tab[:, :, 1, :]
                w0 = i * D
                nc.gpsimd.tensor_tensor(
                    out=ta,
                    in0=cos_t[:],
                    in1=wqk[:, w0 : w0 + D].unsqueeze(1).to_broadcast([P, NA, D]),
                    op=ALU.mult,
                )
                nc.gpsimd.tensor_tensor(
                    out=tb[:, :, 0:64],
                    in0=sin_t[:, :, 64:128],
                    in1=wqk[:, w0 : w0 + 64].unsqueeze(1).to_broadcast([P, NA, 64]),
                    op=ALU.mult,
                )
                nc.gpsimd.tensor_tensor(
                    out=tb[:, :, 64:128],
                    in0=sin_t[:, :, 0:64],
                    in1=wqk[:, w0 + 64 : w0 + D].unsqueeze(1).to_broadcast([P, NA, 64]),
                    op=ALU.mult,
                )
                tabs[nm] = tab

        wts = {}
        wgs = {}
        wcodes = {}

        def w_transpose(unit):
            c, g, bp = unit // 6, (unit % 6) // 2, unit % 2
            wt = psum_t.tile([P, 2, 256], F32, tag="tp")
            for bl in range(2):
                for u in range(2):
                    lo = 256 * g + 128 * u
                    nc.tensor.transpose(
                        wt[:, u, bl * P : (bl + 1) * P],
                        raw[c][:, 2 * bp + bl, :].bitcast(F32)[:, lo : lo + P],
                        ident_f[:],
                    )
            wts[unit] = wt

        def w_copy(unit, eng):
            bp = unit % 2
            if bp == 0:
                wg = grp.tile([P, 2048], BF16, tag="wg", align_bytes=64)
                wgs[unit // 2] = wg
            wg32 = wgs[unit // 2][:].bitcast(F32).rearrange("p (n u) -> p n u", u=2)
            dst = wg32[:, bp * 256 : (bp + 1) * 256, :]
            src = wts[unit][:].rearrange("p u n -> p n u")
            if eng == "s":
                nc.scalar.copy(out=dst, in_=src)
            else:
                nc.vector.tensor_copy(out=dst, in_=src)

        def w_quant(tile_no):
            c, g = tile_no // 3, tile_no % 3
            if g == 0:
                codes = codep.tile([P, NG, 512], U32, tag="codes", align_bytes=64)
                scales = codep.tile([P, NG, 512], U8, tag="scales", align_bytes=64)
                wcodes[c] = (codes, scales)
            codes, scales = wcodes[c]
            nc.vector.quantize_mx(
                out=codes[:, g, :].bitcast(FP8X4), scales=scales[:, g, :], in_=wgs[tile_no][:]
            )

        accs = {}
        rss = {}
        prods = {}

        def mx(slot):
            c, a = slot // NA, slot % NA
            codes, scales = wcodes[c]
            acc = psum_a.tile([P, 512], F32, tag="acc")
            for g in range(NG):
                nc.tensor.matmul_mx(
                    out=acc[:],
                    lhsT=h_codes[:, g, a * P : (a + 1) * P].bitcast(FP8X4),
                    lhsT_scale=h_scales[:, g, a * P : (a + 1) * P],
                    rhs=codes[:, g, :].bitcast(FP8X4),
                    rhs_scale=scales[:, g, :],
                    start=(g == 0),
                    stop=(g == NG - 1),
                )
            accs[slot] = acc

        sss = {}

        def head_squares(slot):
            acc = accs[slot]
            ss = small.tile([P, 4], F32, tag="ss")
            sss[slot] = ss
            for hh in range(4):
                sq = small.tile([P, D], BF16, tag="sq")
                nc.scalar.activation(
                    out=sq[:],
                    in_=acc[:, hh * D : (hh + 1) * D],
                    func=ACT.Square,
                    accum_out=ss[:, hh : hh + 1],
                )

        def head_rsqrt(slot):
            rs = small.tile([P, 4], F32, tag="rs")
            nc.scalar.activation(
                out=rs[:], in_=sss[slot][:], func=ACT.Abs_reciprocal_sqrt, scale=1.0 / D, bias=eps_t[:]
            )
            rss[slot] = rs

        def rope_products(slot):
            c, a = slot // NA, slot % NA
            acc = accs[slot]
            rs = rss[slot]
            tab = tabs["k" if c == NC - 2 else "q"]
            if slot % 2 == 0:
                t12 = ep.tile([P, 4, 2, 2, D], F32, tag="t12")
                prods[slot // 2] = t12
            t12 = prods[slot // 2]
            for hh in range(4):
                nc.vector.scalar_tensor_tensor(
                    out=t12[:, hh, slot % 2, :, :],
                    in0=acc[:, hh * D : (hh + 1) * D].unsqueeze(1).to_broadcast([P, 2, D]),
                    scalar=rs[:, hh : hh + 1],
                    in1=tab[:, a, :, :],
                    op0=ALU.mult,
                    op1=ALU.mult,
                )

        outs = {}

        def out_tile(pair):
            o = outp.tile([P, 4, 2, D], F32, tag="o")
            outs[pair] = o

        def rope_add(pair, i0, i1, eng):
            t12 = prods[pair]
            o = outs[pair]
            if i1 - i0 == 2:
                split = "p h i (f d) -> p (h i) f d"
                eng.tensor_tensor(
                    out=o[:].rearrange(split, f=2),
                    in0=t12[:, :, :, 0, :].rearrange(split, f=2),
                    in1=t12[:, :, :, 1, :].rearrange(split, f=2)[:, :, ::-1, :],
                    op=ALU.add,
                )
                return
            eng.tensor_tensor(
                out=o[:, :, i0:i1, 0:64],
                in0=t12[:, :, i0:i1, 0, 0:64],
                in1=t12[:, :, i0:i1, 1, 64:128],
                op=ALU.add,
            )
            eng.tensor_tensor(
                out=o[:, :, i0:i1, 64:128],
                in0=t12[:, :, i0:i1, 0, 64:128],
                in1=t12[:, :, i0:i1, 1, 0:64],
                op=ALU.add,
            )

        def store(pair, i0, i1):
            c, a = (2 * pair) // NA, (2 * pair) % NA
            src = outs[pair]
            if i1 - i0 == 2:
                nc.sync.dma_start(out=o_dst(c, a, a + 2), in_=src[:].rearrange("p h i d -> p h (i d)"))
            else:
                nc.sync.dma_start(out=o_dst(c, a + i0, a + i1), in_=src[:, :, i0, :])

        def v_copy(slot, eng):
            dst = outs[slot // 2][:, :, slot % 2, :]
            src = accs[slot][:].rearrange("p (h d) -> p h d", d=D)
            if eng == "s":
                nc.scalar.copy(out=dst, in_=src)
            else:
                nc.vector.tensor_copy(out=dst, in_=src)

        def t_units(units):
            for unit in units:
                w_transpose(unit)
                if unit % 6 == 5 and unit // 6 + RAW_BUFS < NC:
                    load_w(unit // 6 + RAW_BUFS)

        def quants_after_run(r):
            if r % 2 == 0:
                w_quant(3 * (r // 2))
            else:
                w_quant(3 * (r // 2) + 1)
                w_quant(3 * (r // 2) + 2)

        def warm_pe(n):
            for i in range(n):
                nc.tensor.matmul(out=wb[3][:], lhsT=ones_b[:], rhs=wrow[:, 0:512], start=True, stop=True)

        def preload_rsqrt():
            nc.scalar.activation(out=warm2[:], in_=eps_t[:], func=ACT.Abs_reciprocal_sqrt)

        for a in range(NA):
            x_square(a)
        h_make(0)
        h_make(1)
        sin_tables()
        w_tables()
        warm_pe(5)
        t_units(range(0, 3))
        warm_pe(3)
        for unit in range(0, 3):
            w_copy(unit, "s")
        h_transpose(0)
        warm_pe(3)
        h_make(2)
        h_make(3)
        for g in range(NG):
            h_copy(0, g, "s")
        quants_after_run(0)
        for g in range(NG):
            h_quant(0, g)
        t_units(range(3, 6))
        warm_pe(3)
        for unit in range(3, 6):
            w_copy(unit, "s")
        quants_after_run(1)
        preload_rsqrt()
        h_transpose(1)
        mx(0)
        mx(1)
        for g in range(NG):
            h_copy(1, g, "v")
        for g in range(NG):
            h_quant(1, g)
        t_units(range(6, 9))

        NPAIR = NC * NA // 2
        NRUN = 2 * NC
        SPLIT_FROM = NRUN - 4
        for m in range(NRUN - 3):
            r = m + 3
            out_tile(m)
            if m == 0:
                head_squares(0)
                head_squares(1)
                head_rsqrt(0)
                head_rsqrt(1)
                for unit in range(6, 9):
                    w_copy(unit, "s")
                t_units(range(9, 12))
                for unit in range(9, 12):
                    w_copy(unit, "s")
                rope_products(0)
                w_quant(3)
                rope_products(1)
                w_quant(4)
                w_quant(5)
            else:
                mx(2 * m)
                t_units((3 * r, 3 * r + 1))
                mx(2 * m + 1)
                t_units((3 * r + 2,))
                head_squares(2 * m)
                w_copy(3 * r, "s")
                head_rsqrt(2 * m)
                rope_products(2 * m)
                if m >= SPLIT_FROM:
                    rope_add(m, 0, 1, nc.gpsimd)
                    store(m, 0, 1)
                if r % 2 == 1:
                    w_quant(3 * (r // 2) + 1)
                head_squares(2 * m + 1)
                w_copy(3 * r + 1, "s")
                head_rsqrt(2 * m + 1)
                w_copy(3 * r + 2, "s")
                rope_products(2 * m + 1)
                w_quant(3 * (r // 2) + (2 if r % 2 == 1 else 0))
            if m >= SPLIT_FROM:
                rope_add(m, 1, 2, nc.gpsimd)
                store(m, 1, 2)
            else:
                rope_add(m, 0, 2, nc.gpsimd)
                store(m, 0, 2)

        m = NRUN - 3
        mx(2 * m)
        mx(2 * m + 1)
        mx(2 * m + 2)
        mx(2 * m + 3)
        for pair in (m, m + 1, m + 2):
            out_tile(pair)
        head_squares(2 * m)
        head_squares(2 * m + 1)
        head_rsqrt(2 * m)
        head_rsqrt(2 * m + 1)
        rope_products(2 * m)
        rope_add(m, 0, 1, nc.vector)
        store(m, 0, 1)
        v_copy(2 * m + 2, "s")
        v_copy(2 * m + 3, "s")
        store(m + 1, 0, 2)
        mx(2 * m + 4)
        mx(2 * m + 5)
        rope_products(2 * m + 1)
        rope_add(m, 1, 2, nc.vector)
        store(m, 1, 2)
        v_copy(2 * m + 4, "s")
        v_copy(2 * m + 5, "s")
        store(m + 2, 0, 2)
